import numpy as np
import ml_dtypes


def mxq(x, axis, fmt="e4m3"):
    dtype, down = {"e4m3": (ml_dtypes.float8_e4m3fn, 7), "e5m2": (ml_dtypes.float8_e5m2, 14)}[fmt]
    v = np.moveaxis(np.asarray(x, np.float32).astype(ml_dtypes.bfloat16).astype(np.float64), axis, -1)
    blocks = v.reshape(v.shape[:-1] + (-1, 32))
    amax = np.abs(blocks).max(-1, keepdims=True)
    byte = np.maximum(np.where(amax > 0, np.frexp(amax)[1] - 1 + 127, 0) - down, 1)
    scale = np.exp2(byte - 127.0)
    codes = (blocks / scale).astype(np.float32).astype(dtype).astype(np.float64)
    return np.moveaxis((codes * scale).reshape(v.shape), -1, axis)


WIDE = False


def mx_kscale(k):
    if not WIDE:
        return np.ones(k)
    levels = np.array([10, -10, 5, -5, 0])
    if k % 512:
        return np.exp2(np.random.permutation(np.resize(levels, k // 32))).repeat(32)
    a = np.empty((k // 512, 16))
    for p in range(k // 512):
        a[p, :8] = np.random.permutation(np.resize(levels, 8))
        for g in range(8):
            far = levels[np.abs(levels - a[p, g]) >= 10]
            a[p, g + 8] = far[np.random.randint(len(far))]
    return np.exp2(a.ravel()).repeat(32)


BF16 = ml_dtypes.bfloat16


def bf(x):
    return np.asarray(x, np.float32).astype(BF16)


def f64(x):
    return np.asarray(x).astype(np.float64)


E2M1 = np.array([0.0, 0.5, 1.0, 1.5, 2.0, 3.0, 4.0, 6.0, -0.0, -0.5, -1.0, -1.5, -2.0, -3.0, -4.0, -6.0])


def pack_weight(w, fmt):
    k, n = w.shape
    w = f64(bf(w)).reshape(k // 32, 32, n)
    amax = np.abs(w).max(1)
    if fmt == "e4m3":
        byte = np.frexp(amax)[1] - 1 + 127 - 7
    else:
        mant, ex = np.frexp(amax / 6.0)
        byte = np.where(mant > 0.5, ex, ex - 1) + 127
    byte = np.clip(np.where(amax > 0, byte, 1), 1, 254)
    scaled = (w * np.exp2(127.0 - byte)[:, None, :]).reshape(k, n).astype(np.float32)
    by_word = np.ascontiguousarray(scaled.reshape(k // 512, 128, 4, n).transpose(0, 1, 3, 2))
    if fmt == "e4m3":
        words = by_word.astype(ml_dtypes.float8_e4m3fn).view(np.uint8)
    else:
        c = by_word.astype(ml_dtypes.float4_e2m1fn).view(np.uint8) & 0xF
        words = c[..., 0::2] | (c[..., 1::2] << 4)
    return np.ascontiguousarray(words), np.ascontiguousarray(byte.astype(np.uint8).reshape(k // 512, 16, n))


def unpack_weight(words, scales, fmt):
    g, p, n, _ = words.shape
    if fmt == "e4m3":
        vals = np.ascontiguousarray(words).view(ml_dtypes.float8_e4m3fn).astype(np.float64)
    else:
        nib = np.empty((g, p, n, 4), np.uint8)
        nib[..., 0::2] = words & 0xF
        nib[..., 1::2] = words >> 4
        vals = E2M1[nib]
    vals = vals * np.repeat(np.exp2(scales.astype(np.float64) - 127.0), 8, axis=1)[..., None]
    return vals.transpose(0, 1, 3, 2).reshape(g * 512, n)
def pack4(w):
    words, scales = pack_weight(w, "e2m1")
    return words.reshape(words.shape[0], 128, -1), scales


def unpack4(words, scales):
    return unpack_weight(words.reshape(words.shape[0], 128, -1, 2), scales, "e2m1")


B, L, C, KS, NL, BH, R = 1, 128, 512, 4, 24, 64, 4
OUT = 2 * BH * NL


def draw0():
    s, t = mx_kscale(C), mx_kscale(C)
    local_features = bf(np.random.standard_normal((B, L, C)) * s)
    wt = bf(np.random.standard_normal((C, C, KS)) / np.sqrt(C) / s[:, None, None] * t[None, :, None])
    bt = bf(np.random.standard_normal(C) * 0.5 * t)
    w1 = np.random.standard_normal((OUT, C)) / np.sqrt(C) / t[None, :]
    w1_words, w1_scales = pack4(np.ascontiguousarray(w1.T))
    return {"local_features": local_features,
            "wt": wt,
            "bt": bt,
            "w1_words": w1_words,
            "w1_scales": w1_scales,
            "b1": bf(np.random.standard_normal(OUT) * 0.5)}


def core(local_features, wt, bt, w1_words, w1_scales, b1):
    xq = mxq(f64(local_features), 2, "e4m3")
    wq = mxq(f64(wt), 0, "e4m3")
    up = xq @ wq.reshape(C, C * KS)
    up = up.reshape(B, L, C, KS).transpose(0, 2, 1, 3).reshape(B, C, L * KS) + f64(bt)[None, :, None]
    y = (unpack4(w1_words, w1_scales).T @ mxq(up, 1, "e4m3")) + f64(b1)[None, :, None]
    y = np.tile(y, (1, 1, R))
    y = y.reshape(B, NL, 2 * BH, L * KS * R)
    return np.ascontiguousarray(y.transpose(2, 0, 1, 3))


def e4m3fn_bytes(y):
    return np.clip(np.asarray(y, np.float64), -448.0, 448.0).astype(np.float32).astype(ml_dtypes.float8_e4m3fn).view(np.uint8)


def e4m3fn_values(b):
    return np.asarray(b, np.uint8).view(ml_dtypes.float8_e4m3fn).astype(np.float64)


def setup_inputs():
    d = draw0()
    x0 = np.asarray(d['local_features']).astype(np.float64)
    s = (np.max(np.abs(x0), axis=(0, 1), keepdims=True) / 448.0).astype(np.float32)
    out = {}
    for k, v in d.items():
        if k == 'local_features':
            out['local_features_bytes'] = e4m3fn_bytes(x0 / s.astype(np.float64))
            out['local_features_scale'] = s
        else:
            out[k] = v
    return out


def reference(local_features_bytes, local_features_scale, wt, bt, w1_words, w1_scales, b1):
    return core(e4m3fn_values(local_features_bytes) * local_features_scale.astype(np.float64), wt, bt, w1_words, w1_scales, b1)

@@ -1,0 +1,225 @@
+from contextlib import ExitStack
+
+import concourse.mybir as mybir
+from concourse.masks import make_identity
+
+P = 128
+C = 512
+L = 128
+KS = 4
+T = 4
+NL = 24
+R = 4
+W = L * KS
+
+F32 = mybir.dt.float32
+BF16 = mybir.dt.bfloat16
+I32 = mybir.dt.int32
+U32 = mybir.dt.uint32
+U8 = mybir.dt.uint8
+FP8 = mybir.dt.float8_e4m3fn
+FP8X4 = mybir.dt.float8_e4m3fn_x4
+FP4X4 = mybir.dt.float4_e2m1fn_x4
+ADD = mybir.AluOpType.add
+MULT = mybir.AluOpType.mult
+IDENTITY = mybir.ActivationFunctionType.Identity
+
+FLOPS = 2 * (L * C * C * KS + NL * 128 * C * W)
+
+QUARTERS = 4
+MQ = P // QUARTERS
+VECTOR_SLOTS = ((0, 1, 2), (0, 1), (0, 1), (0, 1))
+SCALAR_TAP = 1
+
+
+def tile_conditionalfeaturesupsample_w4_kernel(
+    tc, features_bytes, features_scale, wt, bt, w1_words, w1_scales, b1, out
+):
+    nc = tc.nc
+    with ExitStack() as ctx:
+        keep = ctx.enter_context(tc.tile_pool(name="keep", bufs=1))
+        stage = ctx.enter_context(tc.tile_pool(name="stage", bufs=4))
+        psum = ctx.enter_context(tc.psum_pool(name="psum", bufs=6))
+        ctx.enter_context(tc.manual_schedule())
+
+        x_bytes = keep.tile([P, C], U8, align_bytes=64)
+        nc.sync.dma_start(out=x_bytes[:], in_=features_bytes.rearrange("b l c -> (b l) c"))
+        x_scale = keep.tile([P, T], F32)
+        nc.scalar.dma_start(out=x_scale[:], in_=features_scale.rearrange("a b (p t) -> p (a b t)", t=T))
+        bt_sb = keep.tile([P, T], BF16)
+        nc.scalar.dma_start(out=bt_sb[:], in_=bt.rearrange("(p t) -> p t", t=T))
+
+        wt_rows = wt.rearrange("(p j) o k -> p j (o k)", j=T)
+        raw = []
+        for q in range(QUARTERS):
+            raw_q = stage.tile([P, T, MQ * T * KS], BF16, align_bytes=64)
+            nc.sync.dma_start(out=raw_q[:], in_=wt_rows[:, :, q * MQ * T * KS : (q + 1) * MQ * T * KS])
+            raw.append(raw_q)
+
+        ident = keep.tile([P, P], BF16)
+        make_identity(nc, ident[:])
+        planes = keep.tile([P, NL * 128], U8, align_bytes=64)
+        nc.gpsimd.memset(planes[:].bitcast(I32), 0)
+        b1_rows = keep.tile([P, 128], BF16)
+        nc.vector.memset(b1_rows[:], 0.0)
+        nc.scalar.dma_start(out=b1_rows[0:NL, :], in_=b1.rearrange("(n j) -> n j", j=128))
+
+        scale_rows = w1_scales.rearrange("g q n -> (g q) n").bitcast(I32)
+        for quad in range(4):
+            nc.sync.dma_start(
+                out=planes[32 * quad : 32 * quad + 4, :].bitcast(I32), in_=scale_rows[4 * quad : 4 * quad + 4, :]
+            )
+        words = keep.tile([P, 2 * NL * 128], U8, align_bytes=64)
+        nc.sync.dma_start(out=words[:].bitcast(I32), in_=w1_words.rearrange("g p n -> (g p) n").bitcast(I32))
+
+        x_wide = keep.tile([P, C], BF16, align_bytes=64)
+        nc.vector.tensor_copy(out=x_wide[:], in_=x_bytes[:].bitcast(FP8))
+        x_turned = psum.tile([P, T, L], BF16, tag="turn", bufs=2)
+        for t in range(T):
+            nc.tensor.transpose(x_turned[:, t, :], x_wide[:, t::T], ident[:])
+        b1_turned = psum.tile([P, 128], BF16, tag="turn", bufs=2)
+        nc.tensor.transpose(b1_turned[:], b1_rows[:], ident[:])
+
+        x_grouped = keep.tile([P, L, T], BF16, align_bytes=64)
+        x_codes = keep.tile([P, L], U32, align_bytes=64)
+        x_scales = keep.tile([P, L], U8, align_bytes=64)
+
+        grouped = keep.tile([P, KS * T * P * T], BF16, align_bytes=64)
+        grouped_v = grouped[:].rearrange("p (k t m j) -> p k t m j", k=KS, t=T, m=P)
+        w_codes = keep.tile([P, KS * T * P], U32, align_bytes=64)
+        w_scales = keep.tile([P, KS * T * P], U8, align_bytes=64)
+
+        def interleave(q, t):
+            dst = grouped_v[:, :, t, q * MQ : (q + 1) * MQ, :].rearrange("p k m j -> p m k j")
+            src = raw[q][:].rearrange("p j (m t k) -> p t m k j", t=T, k=KS)[:, t]
+            if t in VECTOR_SLOTS[q]:
+                nc.vector.tensor_copy(out=dst, in_=src)
+            else:
+                nc.scalar.copy(out=dst, in_=src)
+
+        def quantize_half(k, half):
+            for t in range(T):
+                c0 = (k * T + t) * P + half * 64
+                nc.vector.quantize_mx(
+                    out=w_codes[:, c0 : c0 + 64].bitcast(FP8X4),
+                    scales=w_scales[:, c0 : c0 + 64],
+                    in_=grouped[:, T * c0 : T * (c0 + 64)],
+                )
+
+        for t in range(T):
+            interleave(0, t)
+        nc.vector.tensor_tensor(
+            out=x_grouped[:],
+            in0=x_turned[:].rearrange("p t l -> p l t"),
+            in1=x_scale[:].unsqueeze(1).to_broadcast([P, L, T]),
+            op=MULT,
+        )
+        b1_cols = keep.tile([P, NL], F32)
+        nc.scalar.copy(out=b1_cols[:], in_=b1_turned[:, 0:NL])
+        for t in range(T):
+            interleave(1, t)
+        nc.vector.quantize_mx(
+            out=x_codes[:].bitcast(FP8X4), scales=x_scales[:], in_=x_grouped[:].rearrange("p l t -> p (l t)")
+        )
+        for k in range(KS):
+            quantize_half(k, 0)
+        for q in (2, 3):
+            for t in range(T):
+                interleave(q, t)
+
+        up_grouped = keep.tile([P, KS, L, T], BF16, align_bytes=64)
+        up_codes = keep.tile([P, KS * L], U32, align_bytes=64)
+        up_scales = keep.tile([P, KS * L], U8, align_bytes=64)
+        up_acc = []
+
+        def multiply(k):
+            acc = psum.tile([P, T, L], F32, tag="acc", bufs=6)
+            for t in range(T):
+                c0 = (k * T + t) * P
+                nc.tensor.matmul_mx(
+                    out=acc[:, t, :],
+                    lhsT=w_codes[:, c0 : c0 + P].bitcast(FP8X4),
+                    lhsT_scale=w_scales[:, c0 : c0 + P],
+                    rhs=x_codes[:].bitcast(FP8X4),
+                    rhs_scale=x_scales[:],
+                    start=True,
+                    stop=True,
+                )
+            up_acc.append(acc)
+
+        def add_bias(k):
+            if k == SCALAR_TAP:
+                for t in range(T):
+                    nc.scalar.activation(
+                        out=up_grouped[:, k, :, t], in_=up_acc[k][:, t, :], func=IDENTITY, bias=bt_sb[:, t : t + 1]
+                    )
+            else:
+                nc.vector.tensor_tensor(
+                    out=up_grouped[:, k],
+                    in0=up_acc[k][:].rearrange("p t l -> p l t"),
+                    in1=bt_sb[:].unsqueeze(1).to_broadcast([P, L, T]),
+                    op=ADD,
+                )
+
+        def quantize_up(k):
+            nc.vector.quantize_mx(
+                out=up_codes[:, k * L : (k + 1) * L].bitcast(FP8X4),
+                scales=up_scales[:, k * L : (k + 1) * L],
+                in_=up_grouped[:, k].rearrange("p l t -> p (l t)"),
+            )
+
+        quantize_half(0, 1)
+        multiply(0)
+        quantize_half(1, 1)
+        multiply(1)
+        quantize_half(2, 1)
+        multiply(2)
+        add_bias(1)
+        add_bias(0)
+        quantize_half(3, 1)
+        multiply(3)
+        add_bias(2)
+        quantize_up(0)
+        add_bias(3)
+        quantize_up(2)
+        quantize_up(1)
+        quantize_up(3)
+
+        out_rows = out.rearrange("j b n x -> j (b n) x")
+
+        def emit(n, dst, copies):
+            acc = psum.tile([P, KS, L], F32, tag="acc", bufs=6)
+            nc.tensor.matmul_mx(
+                out=acc[:].rearrange("p k l -> p (k l)"),
+                lhsT=words[:, 256 * n : 256 * (n + 1)].bitcast(FP4X4),
+                lhsT_scale=planes[:, 128 * n : 128 * (n + 1)],
+                rhs=up_codes[:].bitcast(FP8X4),
+                rhs_scale=up_scales[:],
+                start=True,
+                stop=True,
+            )
+            src = acc[:].rearrange("p k l -> p l k")
+            if copies > 1:
+                src = src.unsqueeze(1).to_broadcast([P, copies, L, KS])
+                dst = dst.rearrange("p (r l k) -> p r l k", r=copies, k=KS)
+            else:
+                dst = dst.rearrange("p (l k) -> p l k", k=KS)
+            if n % 2 == 0:
+                nc.scalar.activation(out=dst, in_=src, func=IDENTITY, bias=b1_cols[:, n : n + 1])
+            else:
+                nc.vector.tensor_scalar(out=dst, in0=src, scalar1=b1_cols[:, n : n + 1], scalar2=None, op0=ADD)
+
+        for n in range(2):
+            y_once = stage.tile([P, W], F32, tag="y_once", bufs=2)
+            emit(n, y_once[:], 1)
+            nc.sync.dma_start(
+                out=out_rows[:, n, :].rearrange("j (r w) -> j r w", r=R),
+                in_=y_once[:].unsqueeze(1).to_broadcast([P, R, W]),
+            )
+        n = 2
+        for size in (2, 4, 4, 4, 4, 4):
+            y_group = stage.tile([P, 4, R * W], F32, tag="y_group", bufs=4)
+            for i in range(size):
+                emit(n + i, y_group[:, i, :], R)
+            nc.sync.dma_start(out=out_rows[:, n : n + size, :], in_=y_group[:, 0:size, :])
+            n += size

@@ -10,6 +10,8 @@ KS = 4
 T = 4
 NL = 24
 R = 4
+HALVES = 2
+LH = L // HALVES
 W = L * KS
 
 F32 = mybir.dt.float32
@@ -26,10 +28,9 @@ IDENTITY = mybir.ActivationFunctionType.Identity
 
 FLOPS = 2 * (L * C * C * KS + NL * 128 * C * W)
 
-QUARTERS = 4
-MQ = P // QUARTERS
-VECTOR_SLOTS = ((0, 1, 2), (0, 1), (0, 1), (0, 1))
-SCALAR_TAP = 1
+CHUNKS = ((0, 32, 3), (32, 32, 2), (64, 64, 2))
+WARM = (0, 4, 3)
+SCALAR_TAP = 0
 
 
 def tile_conditionalfeaturesupsample_w4_kernel(
@@ -51,10 +52,10 @@ def tile_conditionalfeaturesupsample_w4_kernel(
 
         wt_rows = wt.rearrange("(p j) o k -> p j (o k)", j=T)
         raw = []
-        for q in range(QUARTERS):
-            raw_q = stage.tile([P, T, MQ * T * KS], BF16, align_bytes=64)
-            nc.sync.dma_start(out=raw_q[:], in_=wt_rows[:, :, q * MQ * T * KS : (q + 1) * MQ * T * KS])
-            raw.append(raw_q)
+        for m0, count, vector_slots in CHUNKS:
+            raw_c = stage.tile([P, T, count * T * KS], BF16, align_bytes=64, bufs=len(CHUNKS))
+            nc.sync.dma_start(out=raw_c[:], in_=wt_rows[:, :, m0 * T * KS : (m0 + count) * T * KS])
+            raw.append(raw_c)
 
         ident = keep.tile([P, P], BF16)
         make_identity(nc, ident[:])
@@ -89,13 +90,18 @@ def tile_conditionalfeaturesupsample_w4_kernel(
         w_codes = keep.tile([P, KS * T * P], U32, align_bytes=64)
         w_scales = keep.tile([P, KS * T * P], U8, align_bytes=64)
 
-        def interleave(q, t):
-            dst = grouped_v[:, :, t, q * MQ : (q + 1) * MQ, :].rearrange("p k m j -> p m k j")
-            src = raw[q][:].rearrange("p j (m t k) -> p t m k j", t=T, k=KS)[:, t]
-            if t in VECTOR_SLOTS[q]:
-                nc.vector.tensor_copy(out=dst, in_=src)
-            else:
-                nc.scalar.copy(out=dst, in_=src)
+        def interleave(c):
+            m0, count, vector_slots = CHUNKS[c]
+            src = raw[c][:].rearrange("p j (m t k) -> p t m j k", t=T, k=KS)
+            for t in range(T):
+                dst = grouped_v[:, :, t, m0 : m0 + count, :].rearrange("p k m j -> p m j k")
+                if t < vector_slots:
+                    nc.vector.tensor_copy(out=dst, in_=src[:, t])
+                else:
+                    nc.scalar.copy(out=dst, in_=src[:, t])
+            for i in range(WARM[c]):
+                warm = psum.tile([P, 512], F32, tag="turn", bufs=2)
+                nc.tensor.matmul(warm[:], lhsT=ident[:], rhs=raw[c][:, i, 0:512], start=True, stop=True)
 
         def quantize_half(k, half):
             for t in range(T):
@@ -106,30 +112,26 @@ def tile_conditionalfeaturesupsample_w4_kernel(
                     in_=grouped[:, T * c0 : T * (c0 + 64)],
                 )
 
-        for t in range(T):
-            interleave(0, t)
         nc.vector.tensor_tensor(
             out=x_grouped[:],
             in0=x_turned[:].rearrange("p t l -> p l t"),
             in1=x_scale[:].unsqueeze(1).to_broadcast([P, L, T]),
             op=MULT,
         )
+        interleave(0)
         b1_cols = keep.tile([P, NL], F32)
         nc.scalar.copy(out=b1_cols[:], in_=b1_turned[:, 0:NL])
-        for t in range(T):
-            interleave(1, t)
+        interleave(1)
         nc.vector.quantize_mx(
             out=x_codes[:].bitcast(FP8X4), scales=x_scales[:], in_=x_grouped[:].rearrange("p l t -> p (l t)")
         )
         for k in range(KS):
             quantize_half(k, 0)
-        for q in (2, 3):
-            for t in range(T):
-                interleave(q, t)
+        interleave(2)
 
-        up_grouped = keep.tile([P, KS, L, T], BF16, align_bytes=64)
-        up_codes = keep.tile([P, KS * L], U32, align_bytes=64)
-        up_scales = keep.tile([P, KS * L], U8, align_bytes=64)
+        up_grouped = keep.tile([P, HALVES, KS, LH, T], BF16, align_bytes=64)
+        up_codes = keep.tile([P, HALVES * KS * LH], U32, align_bytes=64)
+        up_scales = keep.tile([P, HALVES * KS * LH], U8, align_bytes=64)
         up_acc = []
 
         def multiply(k):
@@ -147,79 +149,97 @@ def tile_conditionalfeaturesupsample_w4_kernel(
                 )
             up_acc.append(acc)
 
-        def add_bias(k):
+        def add_bias(k, half):
+            src = up_acc[k][:, :, half * LH : (half + 1) * LH]
             if k == SCALAR_TAP:
                 for t in range(T):
                     nc.scalar.activation(
-                        out=up_grouped[:, k, :, t], in_=up_acc[k][:, t, :], func=IDENTITY, bias=bt_sb[:, t : t + 1]
+                        out=up_grouped[:, half, k, :, t], in_=src[:, t, :], func=IDENTITY, bias=bt_sb[:, t : t + 1]
                     )
             else:
                 nc.vector.tensor_tensor(
-                    out=up_grouped[:, k],
-                    in0=up_acc[k][:].rearrange("p t l -> p l t"),
-                    in1=bt_sb[:].unsqueeze(1).to_broadcast([P, L, T]),
+                    out=up_grouped[:, half, k],
+                    in0=src.rearrange("p t l -> p l t"),
+                    in1=bt_sb[:].unsqueeze(1).to_broadcast([P, LH, T]),
                     op=ADD,
                 )
 
-        def quantize_up(k):
+        def quantize_up(half):
+            cols = slice(half * KS * LH, (half + 1) * KS * LH)
             nc.vector.quantize_mx(
-                out=up_codes[:, k * L : (k + 1) * L].bitcast(FP8X4),
-                scales=up_scales[:, k * L : (k + 1) * L],
-                in_=up_grouped[:, k].rearrange("p l t -> p (l t)"),
+                out=up_codes[:, cols].bitcast(FP8X4),
+                scales=up_scales[:, cols],
+                in_=up_grouped[:, half].rearrange("p k l t -> p (k l t)"),
             )
 
-        quantize_half(0, 1)
-        multiply(0)
-        quantize_half(1, 1)
-        multiply(1)
-        quantize_half(2, 1)
-        multiply(2)
-        add_bias(1)
-        add_bias(0)
-        quantize_half(3, 1)
-        multiply(3)
-        add_bias(2)
+        for k in range(KS):
+            quantize_half(k, 1)
+            multiply(k)
+        for half in range(HALVES):
+            add_bias(SCALAR_TAP, half)
+        add_bias(1, 0)
+        add_bias(2, 0)
+        add_bias(3, 0)
+        add_bias(1, 1)
         quantize_up(0)
-        add_bias(3)
-        quantize_up(2)
-        quantize_up(1)
-        quantize_up(3)
+        add_bias(2, 1)
+        add_bias(3, 1)
 
-        out_rows = out.rearrange("j b n x -> j (b n) x")
+        out_rows = out.rearrange("j b n (r w) -> j (b n) r w", r=R)
 
-        def emit(n, dst, copies):
-            acc = psum.tile([P, KS, L], F32, tag="acc", bufs=6)
+        def multiply_w1(n, dst, cols):
             nc.tensor.matmul_mx(
-                out=acc[:].rearrange("p k l -> p (k l)"),
+                out=dst,
                 lhsT=words[:, 256 * n : 256 * (n + 1)].bitcast(FP4X4),
                 lhsT_scale=planes[:, 128 * n : 128 * (n + 1)],
-                rhs=up_codes[:].bitcast(FP8X4),
-                rhs_scale=up_scales[:],
+                rhs=up_codes[:, cols].bitcast(FP8X4),
+                rhs_scale=up_scales[:, cols],
                 start=True,
                 stop=True,
             )
-            src = acc[:].rearrange("p k l -> p l k")
-            if copies > 1:
-                src = src.unsqueeze(1).to_broadcast([P, copies, L, KS])
-                dst = dst.rearrange("p (r l k) -> p r l k", r=copies, k=KS)
-            else:
-                dst = dst.rearrange("p (l k) -> p l k", k=KS)
+
+        def empty(n, dst, src):
             if n % 2 == 0:
                 nc.scalar.activation(out=dst, in_=src, func=IDENTITY, bias=b1_cols[:, n : n + 1])
             else:
                 nc.vector.tensor_scalar(out=dst, in0=src, scalar1=b1_cols[:, n : n + 1], scalar2=None, op0=ADD)
 
-        for n in range(2):
-            y_once = stage.tile([P, W], F32, tag="y_once", bufs=2)
-            emit(n, y_once[:], 1)
+        for half in range(HALVES):
+            if half == 1:
+                quantize_up(1)
+            acc_half = psum.tile([P, KS, LH], F32, tag="acc", bufs=6)
+            multiply_w1(0, acc_half[:].rearrange("p k l -> p (k l)"), slice(half * KS * LH, (half + 1) * KS * LH))
+            y_half = stage.tile([P, LH * KS], F32, tag="y_half", bufs=2)
+            empty(0, y_half[:].rearrange("p (l k) -> p l k", k=KS), acc_half[:].rearrange("p k l -> p l k"))
             nc.sync.dma_start(
-                out=out_rows[:, n, :].rearrange("j (r w) -> j r w", r=R),
-                in_=y_once[:].unsqueeze(1).to_broadcast([P, R, W]),
+                out=out_rows[:, 0, :, half * LH * KS : (half + 1) * LH * KS],
+                in_=y_half[:].unsqueeze(1).to_broadcast([P, R, LH * KS]),
             )
+
+        def layer(n):
+            acc = psum.tile([P, HALVES, KS, LH], F32, tag="acc", bufs=6)
+            multiply_w1(n, acc[:].rearrange("p h k l -> p (h k l)"), slice(0, W))
+            return acc
+
+        acc_1 = layer(1)
+        y_once = stage.tile([P, W], F32, tag="y_once", bufs=1)
+        empty(
+            1,
+            y_once[:].rearrange("p (h l k) -> p h l k", h=HALVES, k=KS),
+            acc_1[:].rearrange("p h k l -> p h l k"),
+        )
+        nc.sync.dma_start(out=out_rows[:, 1], in_=y_once[:].unsqueeze(1).to_broadcast([P, R, W]))
+
         n = 2
-        for size in (2, 4, 4, 4, 4, 4):
-            y_group = stage.tile([P, 4, R * W], F32, tag="y_group", bufs=4)
+        for size in (1, 1, 2, 4, 4, 4, 4, 2):
+            y_group = stage.tile([P, 4, R, W], F32, tag="y_group", bufs=4)
             for i in range(size):
-                emit(n + i, y_group[:, i, :], R)
-            nc.sync.dma_start(out=out_rows[:, n : n + size, :], in_=y_group[:, 0:size, :])
+                acc_n = layer(n + i)
+                for half in range(HALVES):
+                    empty(
+                        n + i,
+                        y_group[:, i, :, half * LH * KS : (half + 1) * LH * KS].rearrange("p r (l k) -> p r l k", k=KS),
+                        acc_n[:, half].rearrange("p k l -> p l k").unsqueeze(1).to_broadcast([P, R, LH, KS]),
+                    )
+            nc.sync.dma_start(out=out_rows[:, n : n + size], in_=y_group[:, 0:size])
             n += size

@@ -28,8 +28,9 @@ IDENTITY = mybir.ActivationFunctionType.Identity
 
 FLOPS = 2 * (L * C * C * KS + NL * 128 * C * W)
 
-CHUNKS = ((0, 32, 3), (32, 32, 2), (64, 64, 2))
-WARM = (0, 4, 3)
+CHUNKS = ((0, 16, 2), (16, 16, 2), (32, 32, 2), (64, 32, 2), (96, 32, 2))
+WARM = (0, 0, 3, 3, 0)
+EARLY = 8
 SCALAR_TAP = 0
 
 
@@ -46,9 +47,7 @@ def tile_conditionalfeaturesupsample_w4_kernel(
         x_bytes = keep.tile([P, C], U8, align_bytes=64)
         nc.sync.dma_start(out=x_bytes[:], in_=features_bytes.rearrange("b l c -> (b l) c"))
         x_scale = keep.tile([P, T], F32)
-        nc.scalar.dma_start(out=x_scale[:], in_=features_scale.rearrange("a b (p t) -> p (a b t)", t=T))
-        bt_sb = keep.tile([P, T], BF16)
-        nc.scalar.dma_start(out=bt_sb[:], in_=bt.rearrange("(p t) -> p t", t=T))
+        nc.sync.dma_start(out=x_scale[:], in_=features_scale.rearrange("a b (p t) -> p (a b t)", t=T))
 
         wt_rows = wt.rearrange("(p j) o k -> p j (o k)", j=T)
         raw = []
@@ -59,19 +58,31 @@ def tile_conditionalfeaturesupsample_w4_kernel(
 
         ident = keep.tile([P, P], BF16)
         make_identity(nc, ident[:])
-        planes = keep.tile([P, NL * 128], U8, align_bytes=64)
-        nc.gpsimd.memset(planes[:].bitcast(I32), 0)
+        w1_parts = []
+        for n0, n1 in ((0, EARLY), (EARLY, NL)):
+            codes = keep.tile([P, 256 * (n1 - n0)], U8, align_bytes=64, tag=f"w1_codes_{n0}")
+            scales = keep.tile([P, 128 * (n1 - n0)], U8, align_bytes=64, tag=f"w1_scales_{n0}")
+            nc.gpsimd.memset(scales[:].bitcast(I32), 0)
+            w1_parts.append((n0, n1, codes, scales))
         b1_rows = keep.tile([P, 128], BF16)
         nc.vector.memset(b1_rows[:], 0.0)
-        nc.scalar.dma_start(out=b1_rows[0:NL, :], in_=b1.rearrange("(n j) -> n j", j=128))
+        table = keep.tile([P, 1], F32)
+        nc.scalar.activation(out=table[:], in_=b1_rows[:, 0:1], func=IDENTITY, bias=0.0)
+        bt_sb = keep.tile([P, T], BF16)
+        nc.scalar.dma_start(out=bt_sb[:], in_=bt.rearrange("(p t) -> p t", t=T))
+        b1_layers = b1.rearrange("(n j) -> n j", j=128)
+        for n0, n1 in ((0, 16), (16, NL)):
+            nc.scalar.dma_start(out=b1_rows[n0:n1, :], in_=b1_layers[n0:n1, :])
 
         scale_rows = w1_scales.rearrange("g q n -> (g q) n").bitcast(I32)
-        for quad in range(4):
-            nc.sync.dma_start(
-                out=planes[32 * quad : 32 * quad + 4, :].bitcast(I32), in_=scale_rows[4 * quad : 4 * quad + 4, :]
-            )
-        words = keep.tile([P, 2 * NL * 128], U8, align_bytes=64)
-        nc.sync.dma_start(out=words[:].bitcast(I32), in_=w1_words.rearrange("g p n -> (g p) n").bitcast(I32))
+        word_rows = w1_words.rearrange("g p n -> (g p) n").bitcast(I32)
+        for n0, n1, codes, scales in w1_parts:
+            for quad in range(4):
+                nc.sync.dma_start(
+                    out=scales[32 * quad : 32 * quad + 4, :].bitcast(I32),
+                    in_=scale_rows[4 * quad : 4 * quad + 4, 32 * n0 : 32 * n1],
+                )
+            nc.sync.dma_start(out=codes[:].bitcast(I32), in_=word_rows[:, 64 * n0 : 64 * n1])
 
         x_wide = keep.tile([P, C], BF16, align_bytes=64)
         nc.vector.tensor_copy(out=x_wide[:], in_=x_bytes[:].bitcast(FP8))
@@ -93,61 +104,63 @@ def tile_conditionalfeaturesupsample_w4_kernel(
         def interleave(c):
             m0, count, vector_slots = CHUNKS[c]
             src = raw[c][:].rearrange("p j (m t k) -> p t m j k", t=T, k=KS)
-            for t in range(T):
-                dst = grouped_v[:, :, t, m0 : m0 + count, :].rearrange("p k m j -> p m j k")
-                if t < vector_slots:
-                    nc.vector.tensor_copy(out=dst, in_=src[:, t])
-                else:
-                    nc.scalar.copy(out=dst, in_=src[:, t])
+            dst = grouped_v[:, :, :, m0 : m0 + count, :].rearrange("p k t m j -> p t m j k")
+            nc.vector.tensor_copy(out=dst[:, 0:vector_slots], in_=src[:, 0:vector_slots])
+            for t in range(vector_slots, T):
+                nc.scalar.copy(out=dst[:, t], in_=src[:, t])
             for i in range(WARM[c]):
                 warm = psum.tile([P, 512], F32, tag="turn", bufs=2)
-                nc.tensor.matmul(warm[:], lhsT=ident[:], rhs=raw[c][:, i, 0:512], start=True, stop=True)
+                nc.tensor.matmul(warm[:], lhsT=ident[:], rhs=raw[c][:, i, :], start=True, stop=True)
 
-        def quantize_half(k, half):
-            for t in range(T):
-                c0 = (k * T + t) * P + half * 64
-                nc.vector.quantize_mx(
-                    out=w_codes[:, c0 : c0 + 64].bitcast(FP8X4),
-                    scales=w_scales[:, c0 : c0 + 64],
-                    in_=grouped[:, T * c0 : T * (c0 + 64)],
-                )
+        def quantize_w(k, t, half):
+            c0 = (k * T + t) * P + half * 64
+            nc.vector.quantize_mx(
+                out=w_codes[:, c0 : c0 + 64].bitcast(FP8X4),
+                scales=w_scales[:, c0 : c0 + 64],
+                in_=grouped[:, T * c0 : T * (c0 + 64)],
+            )
 
+        interleave(0)
         nc.vector.tensor_tensor(
             out=x_grouped[:],
             in0=x_turned[:].rearrange("p t l -> p l t"),
             in1=x_scale[:].unsqueeze(1).to_broadcast([P, L, T]),
             op=MULT,
         )
-        interleave(0)
-        b1_cols = keep.tile([P, NL], F32)
-        nc.scalar.copy(out=b1_cols[:], in_=b1_turned[:, 0:NL])
         interleave(1)
         nc.vector.quantize_mx(
             out=x_codes[:].bitcast(FP8X4), scales=x_scales[:], in_=x_grouped[:].rearrange("p l t -> p (l t)")
         )
-        for k in range(KS):
-            quantize_half(k, 0)
         interleave(2)
+        b1_cols = keep.tile([P, NL], F32)
+        nc.scalar.copy(out=b1_cols[:], in_=b1_turned[:, 0:NL])
+        for t in range(T):
+            for k in range(KS):
+                quantize_w(k, t, 0)
+        interleave(3)
+        interleave(4)
 
         up_grouped = keep.tile([P, HALVES, KS, LH, T], BF16, align_bytes=64)
         up_codes = keep.tile([P, HALVES * KS * LH], U32, align_bytes=64)
         up_scales = keep.tile([P, HALVES * KS * LH], U8, align_bytes=64)
         up_acc = []
 
-        def multiply(k):
-            acc = psum.tile([P, T, L], F32, tag="acc", bufs=6)
-            for t in range(T):
-                c0 = (k * T + t) * P
-                nc.tensor.matmul_mx(
-                    out=acc[:, t, :],
-                    lhsT=w_codes[:, c0 : c0 + P].bitcast(FP8X4),
-                    lhsT_scale=w_scales[:, c0 : c0 + P],
-                    rhs=x_codes[:].bitcast(FP8X4),
-                    rhs_scale=x_scales[:],
-                    start=True,
-                    stop=True,
-                )
-            up_acc.append(acc)
+        for k in range(KS):
+            acc_k = psum.tile([P, T, L], F32, tag="acc", bufs=6)
+            up_acc.append(acc_k)
+
+        def finish_w(k, t):
+            quantize_w(k, t, 1)
+            c0 = (k * T + t) * P
+            nc.tensor.matmul_mx(
+                out=up_acc[k][:, t, :],
+                lhsT=w_codes[:, c0 : c0 + P].bitcast(FP8X4),
+                lhsT_scale=w_scales[:, c0 : c0 + P],
+                rhs=x_codes[:].bitcast(FP8X4),
+                rhs_scale=x_scales[:],
+                start=True,
+                stop=True,
+            )
 
         def add_bias(k, half):
             src = up_acc[k][:, :, half * LH : (half + 1) * LH]
@@ -173,8 +186,8 @@ def tile_conditionalfeaturesupsample_w4_kernel(
             )
 
         for k in range(KS):
-            quantize_half(k, 1)
-            multiply(k)
+            for t in range(T):
+                finish_w(k, t)
         for half in range(HALVES):
             add_bias(SCALAR_TAP, half)
         add_bias(1, 0)
@@ -188,10 +201,11 @@ def tile_conditionalfeaturesupsample_w4_kernel(
         out_rows = out.rearrange("j b n (r w) -> j (b n) r w", r=R)
 
         def multiply_w1(n, dst, cols):
+            n0, _, codes, scales = w1_parts[0] if n < EARLY else w1_parts[1]
             nc.tensor.matmul_mx(
                 out=dst,
-                lhsT=words[:, 256 * n : 256 * (n + 1)].bitcast(FP4X4),
-                lhsT_scale=planes[:, 128 * n : 128 * (n + 1)],
+                lhsT=codes[:, 256 * (n - n0) : 256 * (n - n0 + 1)].bitcast(FP4X4),
+                lhsT_scale=scales[:, 128 * (n - n0) : 128 * (n - n0 + 1)],
                 rhs=up_codes[:, cols].bitcast(FP8X4),
                 rhs_scale=up_scales[:, cols],
                 start=True,

@@ -31,6 +31,7 @@ FLOPS = 2 * (L * C * C * KS + NL * 128 * C * W)
 CHUNKS = ((0, 16, 2), (16, 16, 2), (32, 32, 2), (64, 32, 2), (96, 32, 2))
 WARM = (0, 0, 3, 3, 0)
 EARLY = 8
+AHEAD = 3
 SCALAR_TAP = 0
 
 
@@ -70,9 +71,6 @@ def tile_conditionalfeaturesupsample_w4_kernel(
         nc.scalar.activation(out=table[:], in_=b1_rows[:, 0:1], func=IDENTITY, bias=0.0)
         bt_sb = keep.tile([P, T], BF16)
         nc.scalar.dma_start(out=bt_sb[:], in_=bt.rearrange("(p t) -> p t", t=T))
-        b1_layers = b1.rearrange("(n j) -> n j", j=128)
-        for n0, n1 in ((0, 16), (16, NL)):
-            nc.scalar.dma_start(out=b1_rows[n0:n1, :], in_=b1_layers[n0:n1, :])
 
         scale_rows = w1_scales.rearrange("g q n -> (g q) n").bitcast(I32)
         word_rows = w1_words.rearrange("g p n -> (g p) n").bitcast(I32)
@@ -83,14 +81,14 @@ def tile_conditionalfeaturesupsample_w4_kernel(
                     in_=scale_rows[4 * quad : 4 * quad + 4, 32 * n0 : 32 * n1],
                 )
             nc.sync.dma_start(out=codes[:].bitcast(I32), in_=word_rows[:, 64 * n0 : 64 * n1])
+            if n0 == 0:
+                nc.sync.dma_start(out=b1_rows[0:NL, :], in_=b1.rearrange("(n j) -> n j", j=128))
 
         x_wide = keep.tile([P, C], BF16, align_bytes=64)
         nc.vector.tensor_copy(out=x_wide[:], in_=x_bytes[:].bitcast(FP8))
-        x_turned = psum.tile([P, T, L], BF16, tag="turn", bufs=2)
+        turned = psum.tile([P, T + 1, L], BF16, tag="turn", bufs=1)
         for t in range(T):
-            nc.tensor.transpose(x_turned[:, t, :], x_wide[:, t::T], ident[:])
-        b1_turned = psum.tile([P, 128], BF16, tag="turn", bufs=2)
-        nc.tensor.transpose(b1_turned[:], b1_rows[:], ident[:])
+            nc.tensor.transpose(turned[:, t, :], x_wide[:, t::T], ident[:])
 
         x_grouped = keep.tile([P, L, T], BF16, align_bytes=64)
         x_codes = keep.tile([P, L], U32, align_bytes=64)
@@ -101,15 +99,18 @@ def tile_conditionalfeaturesupsample_w4_kernel(
         w_codes = keep.tile([P, KS * T * P], U32, align_bytes=64)
         w_scales = keep.tile([P, KS * T * P], U8, align_bytes=64)
 
+        warm = psum.tile([P, 512], F32, tag="warm", bufs=1)
+
         def interleave(c):
             m0, count, vector_slots = CHUNKS[c]
             src = raw[c][:].rearrange("p j (m t k) -> p t m j k", t=T, k=KS)
             dst = grouped_v[:, :, :, m0 : m0 + count, :].rearrange("p k t m j -> p t m j k")
-            nc.vector.tensor_copy(out=dst[:, 0:vector_slots], in_=src[:, 0:vector_slots])
-            for t in range(vector_slots, T):
-                nc.scalar.copy(out=dst[:, t], in_=src[:, t])
+            for t in range(T):
+                if t < vector_slots:
+                    nc.vector.tensor_copy(out=dst[:, t], in_=src[:, t])
+                else:
+                    nc.scalar.copy(out=dst[:, t], in_=src[:, t])
             for i in range(WARM[c]):
-                warm = psum.tile([P, 512], F32, tag="turn", bufs=2)
                 nc.tensor.matmul(warm[:], lhsT=ident[:], rhs=raw[c][:, i, :], start=True, stop=True)
 
         def quantize_w(k, t, half):
@@ -123,7 +124,7 @@ def tile_conditionalfeaturesupsample_w4_kernel(
         interleave(0)
         nc.vector.tensor_tensor(
             out=x_grouped[:],
-            in0=x_turned[:].rearrange("p t l -> p l t"),
+            in0=turned[:, 0:T, :].rearrange("p t l -> p l t"),
             in1=x_scale[:].unsqueeze(1).to_broadcast([P, L, T]),
             op=MULT,
         )
@@ -132,8 +133,6 @@ def tile_conditionalfeaturesupsample_w4_kernel(
             out=x_codes[:].bitcast(FP8X4), scales=x_scales[:], in_=x_grouped[:].rearrange("p l t -> p (l t)")
         )
         interleave(2)
-        b1_cols = keep.tile([P, NL], F32)
-        nc.scalar.copy(out=b1_cols[:], in_=b1_turned[:, 0:NL])
         for t in range(T):
             for k in range(KS):
                 quantize_w(k, t, 0)
@@ -185,11 +184,18 @@ def tile_conditionalfeaturesupsample_w4_kernel(
                 in_=up_grouped[:, half].rearrange("p k l t -> p (k l t)"),
             )
 
+        own = CHUNKS[-1][2]
+        for k in range(AHEAD):
+            for t in range(own):
+                finish_w(k, t)
         for k in range(KS):
-            for t in range(T):
+            for t in range(own if k < AHEAD else 0, T):
                 finish_w(k, t)
         for half in range(HALVES):
             add_bias(SCALAR_TAP, half)
+        nc.tensor.transpose(turned[:, T, :], b1_rows[:], ident[:])
+        b1_cols = keep.tile([P, NL], F32)
+        nc.scalar.copy(out=b1_cols[:], in_=turned[:, T, 0:NL])
         add_bias(1, 0)
         add_bias(2, 0)
         add_bias(3, 0)

from contextlib import ExitStack

import concourse.mybir as mybir
from concourse.masks import make_identity

P = 128
C = 512
L = 128
KS = 4
T = 4
NL = 24
R = 4
HALVES = 2
LH = L // HALVES
W = L * KS

F32 = mybir.dt.float32
BF16 = mybir.dt.bfloat16
I32 = mybir.dt.int32
U32 = mybir.dt.uint32
U8 = mybir.dt.uint8
FP8 = mybir.dt.float8_e4m3fn
FP8X4 = mybir.dt.float8_e4m3fn_x4
FP4X4 = mybir.dt.float4_e2m1fn_x4
ADD = mybir.AluOpType.add
MULT = mybir.AluOpType.mult
IDENTITY = mybir.ActivationFunctionType.Identity

FLOPS = 2 * (L * C * C * KS + NL * 128 * C * W)

CHUNKS = ((0, 16, 2), (16, 16, 2), (32, 32, 2), (64, 32, 2), (96, 32, 2))
WARM = (0, 0, 3, 3, 0)
EARLY = 8
AHEAD = 3
SCALAR_TAP = 0


def tile_conditionalfeaturesupsample_w4_kernel(
    tc, features_bytes, features_scale, wt, bt, w1_words, w1_scales, b1, out
):
    nc = tc.nc
    with ExitStack() as ctx:
        keep = ctx.enter_context(tc.tile_pool(name="keep", bufs=1))
        stage = ctx.enter_context(tc.tile_pool(name="stage", bufs=4))
        psum = ctx.enter_context(tc.psum_pool(name="psum", bufs=6))
        ctx.enter_context(tc.manual_schedule())

        x_bytes = keep.tile([P, C], U8, align_bytes=64)
        nc.sync.dma_start(out=x_bytes[:], in_=features_bytes.rearrange("b l c -> (b l) c"))
        x_scale = keep.tile([P, T], F32)
        nc.sync.dma_start(out=x_scale[:], in_=features_scale.rearrange("a b (p t) -> p (a b t)", t=T))

        wt_rows = wt.rearrange("(p j) o k -> p j (o k)", j=T)
        raw = []
        for m0, count, vector_slots in CHUNKS:
            raw_c = stage.tile([P, T, count * T * KS], BF16, align_bytes=64, bufs=len(CHUNKS))
            nc.sync.dma_start(out=raw_c[:], in_=wt_rows[:, :, m0 * T * KS : (m0 + count) * T * KS])
            raw.append(raw_c)

        ident = keep.tile([P, P], BF16)
        make_identity(nc, ident[:])
        w1_parts = []
        for n0, n1 in ((0, EARLY), (EARLY, NL)):
            codes = keep.tile([P, 256 * (n1 - n0)], U8, align_bytes=64, tag=f"w1_codes_{n0}")
            scales = keep.tile([P, 128 * (n1 - n0)], U8, align_bytes=64, tag=f"w1_scales_{n0}")
            nc.gpsimd.memset(scales[:].bitcast(I32), 0)
            w1_parts.append((n0, n1, codes, scales))
        b1_rows = keep.tile([P, 128], BF16)
        nc.vector.memset(b1_rows[:], 0.0)
        table = keep.tile([P, 1], F32)
        nc.scalar.activation(out=table[:], in_=b1_rows[:, 0:1], func=IDENTITY, bias=0.0)
        bt_sb = keep.tile([P, T], BF16)
        nc.scalar.dma_start(out=bt_sb[:], in_=bt.rearrange("(p t) -> p t", t=T))

        scale_rows = w1_scales.rearrange("g q n -> (g q) n").bitcast(I32)
        word_rows = w1_words.rearrange("g p n -> (g p) n").bitcast(I32)
        for n0, n1, codes, scales in w1_parts:
            for quad in range(4):
                nc.sync.dma_start(
                    out=scales[32 * quad : 32 * quad + 4, :].bitcast(I32),
                    in_=scale_rows[4 * quad : 4 * quad + 4, 32 * n0 : 32 * n1],
                )
            nc.sync.dma_start(out=codes[:].bitcast(I32), in_=word_rows[:, 64 * n0 : 64 * n1])
            if n0 == 0:
                nc.sync.dma_start(out=b1_rows[0:NL, :], in_=b1.rearrange("(n j) -> n j", j=128))

        x_wide = keep.tile([P, C], BF16, align_bytes=64)
        nc.vector.tensor_copy(out=x_wide[:], in_=x_bytes[:].bitcast(FP8))
        turned = psum.tile([P, T + 1, L], BF16, tag="turn", bufs=1)
        for t in range(T):
            nc.tensor.transpose(turned[:, t, :], x_wide[:, t::T], ident[:])

        x_grouped = keep.tile([P, L, T], BF16, align_bytes=64)
        x_codes = keep.tile([P, L], U32, align_bytes=64)
        x_scales = keep.tile([P, L], U8, align_bytes=64)

        grouped = keep.tile([P, KS * T * P * T], BF16, align_bytes=64)
        grouped_v = grouped[:].rearrange("p (k t m j) -> p k t m j", k=KS, t=T, m=P)
        w_codes = keep.tile([P, KS * T * P], U32, align_bytes=64)
        w_scales = keep.tile([P, KS * T * P], U8, align_bytes=64)

        warm = psum.tile([P, 512], F32, tag="warm", bufs=1)

        def interleave(c):
            m0, count, vector_slots = CHUNKS[c]
            src = raw[c][:].rearrange("p j (m t k) -> p t m j k", t=T, k=KS)
            dst = grouped_v[:, :, :, m0 : m0 + count, :].rearrange("p k t m j -> p t m j k")
            for t in range(T):
                if t < vector_slots:
                    nc.vector.tensor_copy(out=dst[:, t], in_=src[:, t])
                else:
                    nc.scalar.copy(out=dst[:, t], in_=src[:, t])
            for i in range(WARM[c]):
                nc.tensor.matmul(warm[:], lhsT=ident[:], rhs=raw[c][:, i, :], start=True, stop=True)

        def quantize_w(k, t, half):
            c0 = (k * T + t) * P + half * 64
            nc.vector.quantize_mx(
                out=w_codes[:, c0 : c0 + 64].bitcast(FP8X4),
                scales=w_scales[:, c0 : c0 + 64],
                in_=grouped[:, T * c0 : T * (c0 + 64)],
            )

        interleave(0)
        nc.vector.tensor_tensor(
            out=x_grouped[:],
            in0=turned[:, 0:T, :].rearrange("p t l -> p l t"),
            in1=x_scale[:].unsqueeze(1).to_broadcast([P, L, T]),
            op=MULT,
        )
        interleave(1)
        nc.vector.quantize_mx(
            out=x_codes[:].bitcast(FP8X4), scales=x_scales[:], in_=x_grouped[:].rearrange("p l t -> p (l t)")
        )
        interleave(2)
        for t in range(T):
            for k in range(KS):
                quantize_w(k, t, 0)
        interleave(3)
        interleave(4)

        up_grouped = keep.tile([P, HALVES, KS, LH, T], BF16, align_bytes=64)
        up_codes = keep.tile([P, HALVES * KS * LH], U32, align_bytes=64)
        up_scales = keep.tile([P, HALVES * KS * LH], U8, align_bytes=64)
        up_acc = []

        for k in range(KS):
            acc_k = psum.tile([P, T, L], F32, tag="acc", bufs=6)
            up_acc.append(acc_k)

        def finish_w(k, t):
            quantize_w(k, t, 1)
            c0 = (k * T + t) * P
            nc.tensor.matmul_mx(
                out=up_acc[k][:, t, :],
                lhsT=w_codes[:, c0 : c0 + P].bitcast(FP8X4),
                lhsT_scale=w_scales[:, c0 : c0 + P],
                rhs=x_codes[:].bitcast(FP8X4),
                rhs_scale=x_scales[:],
                start=True,
                stop=True,
            )

        def add_bias(k, half):
            src = up_acc[k][:, :, half * LH : (half + 1) * LH]
            if k == SCALAR_TAP:
                for t in range(T):
                    nc.scalar.activation(
                        out=up_grouped[:, half, k, :, t], in_=src[:, t, :], func=IDENTITY, bias=bt_sb[:, t : t + 1]
                    )
            else:
                nc.vector.tensor_tensor(
                    out=up_grouped[:, half, k],
                    in0=src.rearrange("p t l -> p l t"),
                    in1=bt_sb[:].unsqueeze(1).to_broadcast([P, LH, T]),
                    op=ADD,
                )

        def quantize_up(half):
            cols = slice(half * KS * LH, (half + 1) * KS * LH)
            nc.vector.quantize_mx(
                out=up_codes[:, cols].bitcast(FP8X4),
                scales=up_scales[:, cols],
                in_=up_grouped[:, half].rearrange("p k l t -> p (k l t)"),
            )

        own = CHUNKS[-1][2]
        for k in range(AHEAD):
            for t in range(own):
                finish_w(k, t)
        for k in range(KS):
            for t in range(own if k < AHEAD else 0, T):
                finish_w(k, t)
        for half in range(HALVES):
            add_bias(SCALAR_TAP, half)
        nc.tensor.transpose(turned[:, T, :], b1_rows[:], ident[:])
        b1_cols = keep.tile([P, NL], F32)
        nc.scalar.copy(out=b1_cols[:], in_=turned[:, T, 0:NL])
        add_bias(1, 0)
        add_bias(2, 0)
        add_bias(3, 0)
        add_bias(1, 1)
        quantize_up(0)
        add_bias(2, 1)
        add_bias(3, 1)

        out_rows = out.rearrange("j b n (r w) -> j (b n) r w", r=R)

        def multiply_w1(n, dst, cols):
            n0, _, codes, scales = w1_parts[0] if n < EARLY else w1_parts[1]
            nc.tensor.matmul_mx(
                out=dst,
                lhsT=codes[:, 256 * (n - n0) : 256 * (n - n0 + 1)].bitcast(FP4X4),
                lhsT_scale=scales[:, 128 * (n - n0) : 128 * (n - n0 + 1)],
                rhs=up_codes[:, cols].bitcast(FP8X4),
                rhs_scale=up_scales[:, cols],
                start=True,
                stop=True,
            )

        def empty(n, dst, src):
            if n % 2 == 0:
                nc.scalar.activation(out=dst, in_=src, func=IDENTITY, bias=b1_cols[:, n : n + 1])
            else:
                nc.vector.tensor_scalar(out=dst, in0=src, scalar1=b1_cols[:, n : n + 1], scalar2=None, op0=ADD)

        for half in range(HALVES):
            if half == 1:
                quantize_up(1)
            acc_half = psum.tile([P, KS, LH], F32, tag="acc", bufs=6)
            multiply_w1(0, acc_half[:].rearrange("p k l -> p (k l)"), slice(half * KS * LH, (half + 1) * KS * LH))
            y_half = stage.tile([P, LH * KS], F32, tag="y_half", bufs=2)
            empty(0, y_half[:].rearrange("p (l k) -> p l k", k=KS), acc_half[:].rearrange("p k l -> p l k"))
            nc.sync.dma_start(
                out=out_rows[:, 0, :, half * LH * KS : (half + 1) * LH * KS],
                in_=y_half[:].unsqueeze(1).to_broadcast([P, R, LH * KS]),
            )

        def layer(n):
            acc = psum.tile([P, HALVES, KS, LH], F32, tag="acc", bufs=6)
            multiply_w1(n, acc[:].rearrange("p h k l -> p (h k l)"), slice(0, W))
            return acc

        acc_1 = layer(1)
        y_once = stage.tile([P, W], F32, tag="y_once", bufs=1)
        empty(
            1,
            y_once[:].rearrange("p (h l k) -> p h l k", h=HALVES, k=KS),
            acc_1[:].rearrange("p h k l -> p h l k"),
        )
        nc.sync.dma_start(out=out_rows[:, 1], in_=y_once[:].unsqueeze(1).to_broadcast([P, R, W]))

        n = 2
        for size in (1, 1, 2, 4, 4, 4, 4, 2):
            y_group = stage.tile([P, 4, R, W], F32, tag="y_group", bufs=4)
            for i in range(size):
                acc_n = layer(n + i)
                for half in range(HALVES):
                    empty(
                        n + i,
                        y_group[:, i, :, half * LH * KS : (half + 1) * LH * KS].rearrange("p r (l k) -> p r l k", k=KS),
                        acc_n[:, half].rearrange("p k l -> p l k").unsqueeze(1).to_broadcast([P, R, LH, KS]),
                    )
            nc.sync.dma_start(out=out_rows[:, n : n + size], in_=y_group[:, 0:size])
            n += size
